import numpy as np
import ml_dtypes


def mxq(x, axis, fmt="e4m3"):
    dtype, down = {"e4m3": (ml_dtypes.float8_e4m3fn, 7), "e5m2": (ml_dtypes.float8_e5m2, 14)}[fmt]
    v = np.moveaxis(np.asarray(x, np.float32).astype(ml_dtypes.bfloat16).astype(np.float64), axis, -1)
    blocks = v.reshape(v.shape[:-1] + (-1, 32))
    amax = np.abs(blocks).max(-1, keepdims=True)
    byte = np.maximum(np.where(amax > 0, np.frexp(amax)[1] - 1 + 127, 0) - down, 1)
    scale = np.exp2(byte - 127.0)
    codes = (blocks / scale).astype(np.float32).astype(dtype).astype(np.float64)
    return np.moveaxis((codes * scale).reshape(v.shape), -1, axis)


WIDE = False


def mx_kscale(k):
    if not WIDE:
        return np.ones(k)
    levels = np.array([10, -10, 5, -5, 0])
    a = np.random.permutation(np.resize(levels, k // 512 * 4)).reshape(k // 512, 4)
    idx = np.arange(k)
    return np.exp2(a[idx // 512, idx % 128 // 32])


BF16 = ml_dtypes.bfloat16


def bf(x):
    return np.asarray(x, np.float32).astype(BF16)


def f64(x):
    return np.asarray(x).astype(np.float64)


E2M1 = np.array([0.0, 0.5, 1.0, 1.5, 2.0, 3.0, 4.0, 6.0, -0.0, -0.5, -1.0, -1.5, -2.0, -3.0, -4.0, -6.0])


def pack_weight(w, fmt):
    k, n = w.shape
    w = f64(bf(w)).reshape(k // 32, 32, n)
    amax = np.abs(w).max(1)
    if fmt == "e4m3":
        byte = np.frexp(amax)[1] - 1 + 127 - 7
    else:
        mant, ex = np.frexp(amax / 6.0)
        byte = np.where(mant > 0.5, ex, ex - 1) + 127
    byte = np.clip(np.where(amax > 0, byte, 1), 1, 254)
    scaled = (w * np.exp2(127.0 - byte)[:, None, :]).reshape(k, n).astype(np.float32)
    by_word = np.ascontiguousarray(scaled.reshape(k // 512, 128, 4, n).transpose(0, 1, 3, 2))
    if fmt == "e4m3":
        words = by_word.astype(ml_dtypes.float8_e4m3fn).view(np.uint8)
    else:
        c = by_word.astype(ml_dtypes.float4_e2m1fn).view(np.uint8) & 0xF
        words = c[..., 0::2] | (c[..., 1::2] << 4)
    return np.ascontiguousarray(words), np.ascontiguousarray(byte.astype(np.uint8).reshape(k // 512, 16, n))


def unpack_weight(words, scales, fmt):
    g, p, n, _ = words.shape
    if fmt == "e4m3":
        vals = np.ascontiguousarray(words).view(ml_dtypes.float8_e4m3fn).astype(np.float64)
    else:
        nib = np.empty((g, p, n, 4), np.uint8)
        nib[..., 0::2] = words & 0xF
        nib[..., 1::2] = words >> 4
        vals = E2M1[nib]
    vals = vals * np.repeat(np.exp2(scales.astype(np.float64) - 127.0), 8, axis=1)[..., None]
    return vals.transpose(0, 1, 3, 2).reshape(g * 512, n)

def pack4(w):
    words, scales = pack_weight(w, "e2m1")
    return words.reshape(words.shape[0], 128, -1), scales


def unpack4(words, scales):
    return unpack_weight(words.reshape(words.shape[0], 128, -1, 2), scales, "e2m1")


B, H, N, D, DT, NH = 4, 128, 128, 512, 16384, 8


def softmax(v, axis):
    e = np.exp(v - v.max(axis=axis, keepdims=True))
    return e / e.sum(axis=axis, keepdims=True)


def setup_inputs():
    s = mx_kscale(DT)
    cand_topics = bf(np.random.standard_normal((B, N, DT)) * s)
    Wq = np.random.standard_normal((D, DT)) * 2.0 / np.sqrt(DT) / s[None, :]
    Wq_words, Wq_scales = pack4(np.ascontiguousarray(Wq.T))
    bq = bf(np.random.standard_normal(D) * 0.5)
    return {"cand_topics": cand_topics,
            "Wq_words": Wq_words,
            "Wq_scales": Wq_scales,
            "bq": bq}


def reference(cand_topics, Wq_words, Wq_scales, bq):
    q = (mxq(f64(cand_topics), 2, "e4m3") @ unpack4(Wq_words, Wq_scales)) + f64(bq)
    query_weights = softmax(np.sqrt((q ** 2).sum(axis=-1)), 1)
    return q, query_weights

@@ -1,0 +1,204 @@
+from contextlib import ExitStack
+
+import concourse.mybir as mybir
+from concourse.masks import make_identity
+
+F32 = mybir.dt.float32
+BF16 = mybir.dt.bfloat16
+I32 = mybir.dt.int32
+U32 = mybir.dt.uint32
+U8 = mybir.dt.uint8
+FP8X4 = mybir.dt.float8_e4m3fn_x4
+FP4X4 = mybir.dt.float4_e2m1fn_x4
+ACT = mybir.ActivationFunctionType
+ALU = mybir.AluOpType
+AXIS = mybir.AxisListType
+
+P = 128
+USERS = 4
+K = 16384
+FEATURES = 512
+PACK = 4
+K_GROUP = P * PACK
+GROUPS = K // K_GROUP
+
+ROUND_USERS = 2
+ROUND_GROUPS = 4
+SLABS = ROUND_USERS * ROUND_GROUPS
+K_ROUND = ROUND_GROUPS * K_GROUP
+CHUNKS = GROUPS // ROUND_GROUPS
+ROUNDS = CHUNKS * (USERS // ROUND_USERS)
+BANK_SLABS = 2
+ROUND_BANKS = SLABS // BANK_SLABS
+X_AHEAD = 7
+
+FLOPS = 2 * USERS * P * K * FEATURES
+
+
+def tile_candidateaware_clickednewsattention_pa_k_kernel(
+    tc, cand_topics, Wq_words, Wq_scales, bq, out_0, out_1
+):
+    nc = tc.nc
+    with ExitStack() as ctx:
+        ctx.enter_context(tc.manual_schedule())
+        const = ctx.enter_context(tc.tile_pool(name="const", bufs=1))
+        weights = ctx.enter_context(tc.tile_pool(name="weights", bufs=1))
+        x_pool = ctx.enter_context(tc.tile_pool(name="x", bufs=X_AHEAD + 1))
+        work = ctx.enter_context(tc.tile_pool(name="work", bufs=2))
+        results = ctx.enter_context(tc.tile_pool(name="results", bufs=USERS))
+        sums = ctx.enter_context(tc.psum_pool(name="sums", bufs=1))
+        banks = ctx.enter_context(tc.psum_pool(name="banks", bufs=ROUND_BANKS))
+
+        bias_rows = const.tile([P, FEATURES], BF16)
+        nc.vector.memset(bias_rows[:], 0.0)
+        nc.scalar.dma_start(out=bias_rows[0:1, :], in_=bq.rearrange("(o f) -> o f", o=1))
+        ones = const.tile([P, P], BF16)
+        nc.vector.memset(ones[:], 1.0)
+        bias_bank = banks.tile([P, FEATURES], F32, tag="bank")
+        nc.tensor.matmul(out=bias_bank[:], lhsT=ones[:], rhs=bias_rows[:], start=True, stop=True)
+
+        one = const.tile([P, 1], F32)
+        nc.vector.memset(one[:], 1.0)
+        table_warm = const.tile([P, 1], F32)
+        nc.scalar.activation(out=table_warm[:], in_=one[:], func=ACT.Sqrt)
+        bias = const.tile([P, FEATURES], F32)
+        nc.scalar.copy(out=bias[:], in_=bias_bank[:])
+
+        identity = const.tile([P, P], F32)
+        make_identity(nc, identity[:])
+
+        w_words = []
+        w_planes = []
+        for c in range(CHUNKS):
+            words = weights.tile([P, ROUND_GROUPS, 2 * FEATURES], U8, name="w_words%d" % c, align_bytes=64)
+            planes = weights.tile([P, ROUND_GROUPS, FEATURES], U8, name="w_planes%d" % c, align_bytes=64)
+            nc.vector.memset(planes[:].bitcast(I32), 0)
+            w_words.append(words)
+            w_planes.append(planes)
+
+        norms = const.tile([P, P], F32)
+        nc.vector.memset(norms[:], 0.0)
+        sum_squares = const.tile([P, USERS], F32)
+
+        q_sums = []
+        for user in range(USERS):
+            q_sum = sums.tile([P, FEATURES], F32, name="q_sum%d" % user)
+            q_sums.append(q_sum)
+
+        words_i32 = Wq_words.bitcast(I32)
+        scales_i32 = Wq_scales.bitcast(I32)
+
+        x_raw = {}
+        x_grouped = {}
+        x_codes = {}
+        x_planes = {}
+
+        def load(i):
+            chunk, pair = divmod(i, USERS // ROUND_USERS)
+            raw = x_pool.tile([P, ROUND_USERS * K_ROUND], BF16)
+            nc.sync.dma_start(
+                out=raw[:].rearrange("n (b k) -> n b k", b=ROUND_USERS),
+                in_=cand_topics[
+                    pair * ROUND_USERS : (pair + 1) * ROUND_USERS, :, chunk * K_ROUND : (chunk + 1) * K_ROUND
+                ].rearrange("b n k -> n b k"),
+            )
+            x_raw[i] = raw
+            if pair == 1:
+                groups = slice(chunk * ROUND_GROUPS, (chunk + 1) * ROUND_GROUPS)
+                for r in range(4):
+                    nc.sync.dma_start(
+                        out=w_planes[chunk][r:P:32, :, :].bitcast(I32),
+                        in_=scales_i32[groups, r:16:4, :].rearrange("g j n -> j g n"),
+                    )
+                nc.sync.dma_start(
+                    out=w_words[chunk][:].bitcast(I32),
+                    in_=words_i32[groups, :, :].rearrange("g p b -> p g b"),
+                )
+
+        def transpose(i):
+            x_sorted = work.tile([P, SLABS, 2, P], F32)
+            nc.vector.tensor_copy(
+                out=x_sorted[:],
+                in_=x_raw[i][:].bitcast(F32).rearrange("n (s p u) -> n s u p", s=SLABS, u=2),
+            )
+            grouped = work.tile([P, SLABS * P * PACK], BF16, align_bytes=64)
+            grouped_words = grouped[:].bitcast(F32).rearrange("p (s n u) -> p s n u", s=SLABS, u=2)
+            for j in range(ROUND_BANKS):
+                bank = banks.tile([P, BANK_SLABS, 2, P], F32, tag="bank")
+                for s in range(BANK_SLABS):
+                    for u in range(2):
+                        nc.tensor.transpose(
+                            out=bank[:, s, u, :], in_=x_sorted[:, j * BANK_SLABS + s, u, :], identity=identity[:]
+                        )
+                nc.scalar.copy(
+                    out=grouped_words[:, j * BANK_SLABS : (j + 1) * BANK_SLABS, :, :],
+                    in_=bank[:].rearrange("p s u n -> p s n u"),
+                )
+            x_grouped[i] = grouped
+
+        def quantise(i):
+            codes = work.tile([P, SLABS * P], U32, align_bytes=64)
+            planes = work.tile([P, SLABS * P], U8, align_bytes=64)
+            nc.vector.quantize_mx(out=codes[:].bitcast(FP8X4), scales=planes[:], in_=x_grouped[i][:])
+            x_codes[i] = codes
+            x_planes[i] = planes
+
+        def multiply(i):
+            chunk, pair = divmod(i, USERS // ROUND_USERS)
+            for s in range(SLABS):
+                b, g = divmod(s, ROUND_GROUPS)
+                group = chunk * ROUND_GROUPS + g
+                candidates = slice(s * P, (s + 1) * P)
+                nc.tensor.matmul_mx(
+                    out=q_sums[pair * ROUND_USERS + b][:],
+                    lhsT=x_codes[i][:, candidates].bitcast(FP8X4),
+                    lhsT_scale=x_planes[i][:, candidates],
+                    rhs=w_words[chunk][:, g, :].bitcast(FP4X4),
+                    rhs_scale=w_planes[chunk][:, g, :],
+                    start=(group == 0),
+                    stop=(group == GROUPS - 1),
+                )
+
+        def finish(user):
+            q = results.tile([P, FEATURES], F32)
+            nc.vector.tensor_tensor(out=q[:], in0=q_sums[user][:], in1=bias[:], op=ALU.add)
+            nc.sync.dma_start(out=out_0[user, :, :], in_=q[:])
+            squares = results.tile([P, FEATURES], F32)
+            nc.scalar.activation(
+                out=squares[:], in_=q[:], func=ACT.Square, accum_out=sum_squares[:, user : user + 1]
+            )
+
+        for i in range(X_AHEAD):
+            load(i)
+        transpose(0)
+        for i in range(1, ROUNDS):
+            if i + X_AHEAD - 1 < ROUNDS:
+                load(i + X_AHEAD - 1)
+            transpose(i)
+            quantise(i - 1)
+            multiply(i - 1)
+        quantise(ROUNDS - 1)
+        for user in range(ROUND_USERS):
+            finish(user)
+        multiply(ROUNDS - 1)
+        for user in range(ROUND_USERS, USERS):
+            finish(user)
+
+        nc.scalar.activation(out=norms[:, 0:USERS], in_=sum_squares[:], func=ACT.Sqrt)
+        nc.scalar.activation(out=table_warm[:], in_=one[:], func=ACT.Exp)
+        norms_bank = banks.tile([P, P], F32, tag="bank")
+        nc.tensor.transpose(out=norms_bank[:], in_=norms[:], identity=identity[:])
+        top = const.tile([P, 1], F32)
+        nc.vector.reduce_max(out=top[:], in_=norms_bank[:], axis=AXIS.X)
+        minus_top = const.tile([P, 1], F32)
+        nc.vector.tensor_scalar_mul(out=minus_top[:], in0=top[:], scalar1=-1.0)
+        powers = const.tile([P, P], F32)
+        total = const.tile([P, 1], F32)
+        nc.scalar.activation(
+            out=powers[:], in_=norms_bank[:], func=ACT.Exp, bias=minus_top[:], scale=1.0, accum_out=total[:]
+        )
+        inverse = const.tile([P, 1], F32)
+        nc.vector.reciprocal(out=inverse[:], in_=total[:])
+        query_weights = const.tile([P, P], F32)
+        nc.vector.tensor_scalar_mul(out=query_weights[:], in0=powers[:], scalar1=inverse[:])
+        nc.sync.dma_start(out=out_1[:, :], in_=query_weights[0:USERS, :])

@@ -21,16 +21,18 @@ FEATURES = 512
 PACK = 4
 K_GROUP = P * PACK
 GROUPS = K // K_GROUP
+SCALE_ROWS = K_GROUP // 32
+QUADRANT = 32
+QUADRANT_ROWS = SCALE_ROWS // (P // QUADRANT)
 
-ROUND_USERS = 2
-ROUND_GROUPS = 4
-SLABS = ROUND_USERS * ROUND_GROUPS
-K_ROUND = ROUND_GROUPS * K_GROUP
-CHUNKS = GROUPS // ROUND_GROUPS
-ROUNDS = CHUNKS * (USERS // ROUND_USERS)
-BANK_SLABS = 2
-ROUND_BANKS = SLABS // BANK_SLABS
-X_AHEAD = 7
+UNIT_GROUPS = 4
+K_UNIT = UNIT_GROUPS * K_GROUP
+CHUNKS = GROUPS // UNIT_GROUPS
+UNITS = CHUNKS * USERS
+BANK_GROUPS = 2
+UNIT_BANKS = UNIT_GROUPS // BANK_GROUPS
+RUN = 2
+X_AHEAD = 14
 
 FLOPS = 2 * USERS * P * K * FEATURES
 
@@ -44,10 +46,10 @@ def tile_candidateaware_clickednewsattention_pa_k_kernel(
         const = ctx.enter_context(tc.tile_pool(name="const", bufs=1))
         weights = ctx.enter_context(tc.tile_pool(name="weights", bufs=1))
         x_pool = ctx.enter_context(tc.tile_pool(name="x", bufs=X_AHEAD + 1))
-        work = ctx.enter_context(tc.tile_pool(name="work", bufs=2))
+        work = ctx.enter_context(tc.tile_pool(name="work", bufs=2 * RUN))
         results = ctx.enter_context(tc.tile_pool(name="results", bufs=USERS))
         sums = ctx.enter_context(tc.psum_pool(name="sums", bufs=1))
-        banks = ctx.enter_context(tc.psum_pool(name="banks", bufs=ROUND_BANKS))
+        banks = ctx.enter_context(tc.psum_pool(name="banks", bufs=RUN * UNIT_BANKS))
 
         bias_rows = const.tile([P, FEATURES], BF16)
         nc.vector.memset(bias_rows[:], 0.0)
@@ -67,15 +69,6 @@ def tile_candidateaware_clickednewsattention_pa_k_kernel(
         identity = const.tile([P, P], F32)
         make_identity(nc, identity[:])
 
-        w_words = []
-        w_planes = []
-        for c in range(CHUNKS):
-            words = weights.tile([P, ROUND_GROUPS, 2 * FEATURES], U8, name="w_words%d" % c, align_bytes=64)
-            planes = weights.tile([P, ROUND_GROUPS, FEATURES], U8, name="w_planes%d" % c, align_bytes=64)
-            nc.vector.memset(planes[:].bitcast(I32), 0)
-            w_words.append(words)
-            w_planes.append(planes)
-
         norms = const.tile([P, P], F32)
         nc.vector.memset(norms[:], 0.0)
         sum_squares = const.tile([P, USERS], F32)
@@ -88,71 +81,72 @@ def tile_candidateaware_clickednewsattention_pa_k_kernel(
         words_i32 = Wq_words.bitcast(I32)
         scales_i32 = Wq_scales.bitcast(I32)
 
+        w_words = {}
+        w_planes = {}
         x_raw = {}
         x_grouped = {}
         x_codes = {}
         x_planes = {}
 
-        def load(i):
-            chunk, pair = divmod(i, USERS // ROUND_USERS)
-            raw = x_pool.tile([P, ROUND_USERS * K_ROUND], BF16)
-            nc.sync.dma_start(
-                out=raw[:].rearrange("n (b k) -> n b k", b=ROUND_USERS),
-                in_=cand_topics[
-                    pair * ROUND_USERS : (pair + 1) * ROUND_USERS, :, chunk * K_ROUND : (chunk + 1) * K_ROUND
-                ].rearrange("b n k -> n b k"),
-            )
-            x_raw[i] = raw
-            if pair == 1:
-                groups = slice(chunk * ROUND_GROUPS, (chunk + 1) * ROUND_GROUPS)
-                for r in range(4):
-                    nc.sync.dma_start(
-                        out=w_planes[chunk][r:P:32, :, :].bitcast(I32),
-                        in_=scales_i32[groups, r:16:4, :].rearrange("g j n -> j g n"),
-                    )
+        def load_weights(chunk):
+            groups = slice(chunk * UNIT_GROUPS, (chunk + 1) * UNIT_GROUPS)
+            words = weights.tile([P, UNIT_GROUPS, 2 * FEATURES], U8, name="w_words%d" % chunk, align_bytes=64)
+            planes = weights.tile([P, UNIT_GROUPS, FEATURES], U8, name="w_planes%d" % chunk, align_bytes=64)
+            nc.vector.memset(planes[:].bitcast(I32), 0)
+            for r in range(QUADRANT_ROWS):
                 nc.sync.dma_start(
-                    out=w_words[chunk][:].bitcast(I32),
-                    in_=words_i32[groups, :, :].rearrange("g p b -> p g b"),
+                    out=planes[r:P:QUADRANT, :, :].bitcast(I32),
+                    in_=scales_i32[groups, r:SCALE_ROWS:QUADRANT_ROWS, :].rearrange("g j n -> j g n"),
                 )
+            nc.sync.dma_start(out=words[:].bitcast(I32), in_=words_i32[groups, :, :].rearrange("g p b -> p g b"))
+            w_words[chunk] = words
+            w_planes[chunk] = planes
 
-        def transpose(i):
-            x_sorted = work.tile([P, SLABS, 2, P], F32)
+        def load(j):
+            chunk, user = divmod(j, USERS)
+            raw = x_pool.tile([P, K_UNIT], BF16)
+            nc.sync.dma_start(out=raw[:], in_=cand_topics[user, :, chunk * K_UNIT : (chunk + 1) * K_UNIT])
+            x_raw[j] = raw
+            if user == USERS - 1:
+                load_weights(chunk)
+
+        def transpose(j):
+            x_sorted = work.tile([P, UNIT_GROUPS, 2, P], F32)
             nc.vector.tensor_copy(
                 out=x_sorted[:],
-                in_=x_raw[i][:].bitcast(F32).rearrange("n (s p u) -> n s u p", s=SLABS, u=2),
+                in_=x_raw[j][:].bitcast(F32).rearrange("n (g p u) -> n g u p", g=UNIT_GROUPS, u=2),
             )
-            grouped = work.tile([P, SLABS * P * PACK], BF16, align_bytes=64)
-            grouped_words = grouped[:].bitcast(F32).rearrange("p (s n u) -> p s n u", s=SLABS, u=2)
-            for j in range(ROUND_BANKS):
-                bank = banks.tile([P, BANK_SLABS, 2, P], F32, tag="bank")
-                for s in range(BANK_SLABS):
+            grouped = work.tile([P, UNIT_GROUPS * P * PACK], BF16, align_bytes=64)
+            grouped_words = grouped[:].bitcast(F32).rearrange("p (g n u) -> p g n u", g=UNIT_GROUPS, u=2)
+            for first_group in range(0, UNIT_GROUPS, BANK_GROUPS):
+                bank = banks.tile([P, BANK_GROUPS, 2, P], F32, tag="bank")
+                for g in range(BANK_GROUPS):
                     for u in range(2):
                         nc.tensor.transpose(
-                            out=bank[:, s, u, :], in_=x_sorted[:, j * BANK_SLABS + s, u, :], identity=identity[:]
+                            out=bank[:, g, u, :], in_=x_sorted[:, first_group + g, u, :], identity=identity[:]
                         )
                 nc.scalar.copy(
-                    out=grouped_words[:, j * BANK_SLABS : (j + 1) * BANK_SLABS, :, :],
-                    in_=bank[:].rearrange("p s u n -> p s n u"),
+                    out=grouped_words[:, first_group : first_group + BANK_GROUPS, :, :],
+                    in_=bank[:].rearrange("p g u n -> p g n u"),
                 )
-            x_grouped[i] = grouped
+            x_grouped[j] = grouped
 
-        def quantise(i):
-            codes = work.tile([P, SLABS * P], U32, align_bytes=64)
-            planes = work.tile([P, SLABS * P], U8, align_bytes=64)
-            nc.vector.quantize_mx(out=codes[:].bitcast(FP8X4), scales=planes[:], in_=x_grouped[i][:])
-            x_codes[i] = codes
-            x_planes[i] = planes
+        def quantise(j):
+            codes = work.tile([P, UNIT_GROUPS * P], U32, align_bytes=64)
+            planes = work.tile([P, UNIT_GROUPS * P], U8, align_bytes=64)
+            nc.vector.quantize_mx(out=codes[:].bitcast(FP8X4), scales=planes[:], in_=x_grouped[j][:])
+            x_codes[j] = codes
+            x_planes[j] = planes
 
-        def multiply(i):
-            chunk, pair = divmod(i, USERS // ROUND_USERS)
-            for s in range(SLABS):
-                b, g = divmod(s, ROUND_GROUPS)
-                group = chunk * ROUND_GROUPS + g
-                candidates = slice(s * P, (s + 1) * P)
+        def multiply(j):
+            chunk, user = divmod(j, USERS)
+            for g in range(UNIT_GROUPS):
+                group = chunk * UNIT_GROUPS + g
+                candidates = slice(g * P, (g + 1) * P)
                 nc.tensor.matmul_mx(
-                    out=q_sums[pair * ROUND_USERS + b][:],
-                    lhsT=x_codes[i][:, candidates].bitcast(FP8X4),
-                    lhsT_scale=x_planes[i][:, candidates],
+                    out=q_sums[user][:],
+                    lhsT=x_codes[j][:, candidates].bitcast(FP8X4),
+                    lhsT_scale=x_planes[j][:, candidates],
                     rhs=w_words[chunk][:, g, :].bitcast(FP4X4),
                     rhs_scale=w_planes[chunk][:, g, :],
                     start=(group == 0),
@@ -168,30 +162,30 @@ def tile_candidateaware_clickednewsattention_pa_k_kernel(
                 out=squares[:], in_=q[:], func=ACT.Square, accum_out=sum_squares[:, user : user + 1]
             )
 
-        for i in range(X_AHEAD):
-            load(i)
-        transpose(0)
-        for i in range(1, ROUNDS):
-            if i + X_AHEAD - 1 < ROUNDS:
-                load(i + X_AHEAD - 1)
-            transpose(i)
-            quantise(i - 1)
-            multiply(i - 1)
-        quantise(ROUNDS - 1)
-        for user in range(ROUND_USERS):
-            finish(user)
-        multiply(ROUNDS - 1)
-        for user in range(ROUND_USERS, USERS):
-            finish(user)
+        def run_units(first):
+            return [j for j in range(first, first + RUN) if 0 <= j < UNITS]
+
+        for j in range(X_AHEAD):
+            load(j)
+        for first in range(0, UNITS + 2 * RUN, RUN):
+            for j in run_units(first):
+                if j + X_AHEAD < UNITS:
+                    load(j + X_AHEAD)
+                transpose(j)
+            for j in run_units(first - RUN):
+                quantise(j)
+            for j in run_units(first - 2 * RUN):
+                if j // USERS == CHUNKS - 1:
+                    finish(j % USERS)
+            for j in run_units(first - RUN):
+                multiply(j)
 
         nc.scalar.activation(out=norms[:, 0:USERS], in_=sum_squares[:], func=ACT.Sqrt)
         nc.scalar.activation(out=table_warm[:], in_=one[:], func=ACT.Exp)
         norms_bank = banks.tile([P, P], F32, tag="bank")
         nc.tensor.transpose(out=norms_bank[:], in_=norms[:], identity=identity[:])
-        top = const.tile([P, 1], F32)
-        nc.vector.reduce_max(out=top[:], in_=norms_bank[:], axis=AXIS.X)
         minus_top = const.tile([P, 1], F32)
-        nc.vector.tensor_scalar_mul(out=minus_top[:], in0=top[:], scalar1=-1.0)
+        nc.vector.reduce_max(out=minus_top[:], in_=norms_bank[:], axis=AXIS.X, negate=True)
         powers = const.tile([P, P], F32)
         total = const.tile([P, 1], F32)
         nc.scalar.activation(

@@ -51,20 +51,10 @@ def tile_candidateaware_clickednewsattention_pa_k_kernel(
         sums = ctx.enter_context(tc.psum_pool(name="sums", bufs=1))
         banks = ctx.enter_context(tc.psum_pool(name="banks", bufs=RUN * UNIT_BANKS))
 
-        bias_rows = const.tile([P, FEATURES], BF16)
-        nc.vector.memset(bias_rows[:], 0.0)
-        nc.scalar.dma_start(out=bias_rows[0:1, :], in_=bq.rearrange("(o f) -> o f", o=1))
-        ones = const.tile([P, P], BF16)
-        nc.vector.memset(ones[:], 1.0)
-        bias_bank = banks.tile([P, FEATURES], F32, tag="bank")
-        nc.tensor.matmul(out=bias_bank[:], lhsT=ones[:], rhs=bias_rows[:], start=True, stop=True)
-
         one = const.tile([P, 1], F32)
         nc.vector.memset(one[:], 1.0)
         table_warm = const.tile([P, 1], F32)
         nc.scalar.activation(out=table_warm[:], in_=one[:], func=ACT.Sqrt)
-        bias = const.tile([P, FEATURES], F32)
-        nc.scalar.copy(out=bias[:], in_=bias_bank[:])
 
         identity = const.tile([P, P], F32)
         make_identity(nc, identity[:])
@@ -72,6 +62,7 @@ def tile_candidateaware_clickednewsattention_pa_k_kernel(
         norms = const.tile([P, P], F32)
         nc.vector.memset(norms[:], 0.0)
         sum_squares = const.tile([P, USERS], F32)
+        bias = const.tile([P, FEATURES], BF16)
 
         q_sums = []
         for user in range(USERS):
@@ -109,6 +100,8 @@ def tile_candidateaware_clickednewsattention_pa_k_kernel(
             x_raw[j] = raw
             if user == USERS - 1:
                 load_weights(chunk)
+            if j == UNITS - 1:
+                nc.sync.dma_start(out=bias[:], in_=bq.partition_broadcast(P))
 
         def transpose(j):
             x_sorted = work.tile([P, UNIT_GROUPS, 2, P], F32)

@@ -33,6 +33,8 @@ BANK_GROUPS = 2
 UNIT_BANKS = UNIT_GROUPS // BANK_GROUPS
 RUN = 2
 X_AHEAD = 14
+WARM_FIRST = 6
+WARM_BETWEEN = 2
 
 FLOPS = 2 * USERS * P * K * FEATURES
 
@@ -63,11 +65,17 @@ def tile_candidateaware_clickednewsattention_pa_k_kernel(
         nc.vector.memset(norms[:], 0.0)
         sum_squares = const.tile([P, USERS], F32)
         bias = const.tile([P, FEATURES], BF16)
+        zeros = const.tile([P, FEATURES], BF16)
+        nc.vector.memset(zeros[:], 0.0)
 
         q_sums = []
         for user in range(USERS):
             q_sum = sums.tile([P, FEATURES], F32, name="q_sum%d" % user)
             q_sums.append(q_sum)
+
+        def keep_warm(count):
+            for repeat in range(count):
+                nc.tensor.matmul(out=q_sums[USERS - 1][:], lhsT=zeros[:, 0:P], rhs=zeros[:], start=True, stop=True)
 
         words_i32 = Wq_words.bitcast(I32)
         scales_i32 = Wq_scales.bitcast(I32)
@@ -160,11 +168,14 @@ def tile_candidateaware_clickednewsattention_pa_k_kernel(
 
         for j in range(X_AHEAD):
             load(j)
+        keep_warm(WARM_FIRST)
         for first in range(0, UNITS + 2 * RUN, RUN):
             for j in run_units(first):
                 if j + X_AHEAD < UNITS:
                     load(j + X_AHEAD)
                 transpose(j)
+                if j < USERS:
+                    keep_warm(WARM_BETWEEN)
             for j in run_units(first - RUN):
                 quantise(j)
             for j in run_units(first - 2 * RUN):

@@ -56,7 +56,9 @@ def tile_candidateaware_clickednewsattention_pa_k_kernel(
         one = const.tile([P, 1], F32)
         nc.vector.memset(one[:], 1.0)
         table_warm = const.tile([P, 1], F32)
-        nc.scalar.activation(out=table_warm[:], in_=one[:], func=ACT.Sqrt)
+        nc.scalar.activation(out=table_warm[:], in_=one[:], func=ACT.Exp)
+        half = const.tile([P, 1], F32)
+        nc.vector.memset(half[:], 0.5)
 
         identity = const.tile([P, P], F32)
         make_identity(nc, identity[:])
@@ -162,6 +164,9 @@ def tile_candidateaware_clickednewsattention_pa_k_kernel(
             nc.scalar.activation(
                 out=squares[:], in_=q[:], func=ACT.Square, accum_out=sum_squares[:, user : user + 1]
             )
+            nc.gpsimd.tensor_tensor(
+                out=norms[:, user : user + 1], in0=sum_squares[:, user : user + 1], in1=half[:], op=ALU.pow
+            )
 
         def run_units(first):
             return [j for j in range(first, first + RUN) if 0 <= j < UNITS]
@@ -184,8 +189,6 @@ def tile_candidateaware_clickednewsattention_pa_k_kernel(
             for j in run_units(first - RUN):
                 multiply(j)
 
-        nc.scalar.activation(out=norms[:, 0:USERS], in_=sum_squares[:], func=ACT.Sqrt)
-        nc.scalar.activation(out=table_warm[:], in_=one[:], func=ACT.Exp)
         norms_bank = banks.tile([P, P], F32, tag="bank")
         nc.tensor.transpose(out=norms_bank[:], in_=norms[:], identity=identity[:])
         minus_top = const.tile([P, 1], F32)

@@ -91,8 +91,8 @@ def tile_candidateaware_clickednewsattention_pa_k_kernel(
 
         def load_weights(chunk):
             groups = slice(chunk * UNIT_GROUPS, (chunk + 1) * UNIT_GROUPS)
-            words = weights.tile([P, UNIT_GROUPS, 2 * FEATURES], U8, name="w_words%d" % chunk, align_bytes=64)
-            planes = weights.tile([P, UNIT_GROUPS, FEATURES], U8, name="w_planes%d" % chunk, align_bytes=64)
+            words = weights.tile([P, UNIT_GROUPS, 2 * FEATURES], U8, name="w_words%d" % chunk, align_bytes=256)
+            planes = weights.tile([P, UNIT_GROUPS, FEATURES], U8, name="w_planes%d" % chunk, align_bytes=256)
             nc.vector.memset(planes[:].bitcast(I32), 0)
             for r in range(QUADRANT_ROWS):
                 nc.sync.dma_start(
@@ -119,7 +119,7 @@ def tile_candidateaware_clickednewsattention_pa_k_kernel(
                 out=x_sorted[:],
                 in_=x_raw[j][:].bitcast(F32).rearrange("n (g p u) -> n g u p", g=UNIT_GROUPS, u=2),
             )
-            grouped = work.tile([P, UNIT_GROUPS * P * PACK], BF16, align_bytes=64)
+            grouped = work.tile([P, UNIT_GROUPS * P * PACK], BF16, align_bytes=256)
             grouped_words = grouped[:].bitcast(F32).rearrange("p (g n u) -> p g n u", g=UNIT_GROUPS, u=2)
             for first_group in range(0, UNIT_GROUPS, BANK_GROUPS):
                 bank = banks.tile([P, BANK_GROUPS, 2, P], F32, tag="bank")
@@ -135,8 +135,8 @@ def tile_candidateaware_clickednewsattention_pa_k_kernel(
             x_grouped[j] = grouped
 
         def quantise(j):
-            codes = work.tile([P, UNIT_GROUPS * P], U32, align_bytes=64)
-            planes = work.tile([P, UNIT_GROUPS * P], U8, align_bytes=64)
+            codes = work.tile([P, UNIT_GROUPS * P], U32, align_bytes=256)
+            planes = work.tile([P, UNIT_GROUPS * P], U8, align_bytes=256)
             nc.vector.quantize_mx(out=codes[:].bitcast(FP8X4), scales=planes[:], in_=x_grouped[j][:])
             x_codes[j] = codes
             x_planes[j] = planes

@@ -60,7 +60,7 @@ def tile_candidateaware_clickednewsattention_pa_k_kernel(
         half = const.tile([P, 1], F32)
         nc.vector.memset(half[:], 0.5)
 
-        identity = const.tile([P, P], F32)
+        identity = const.tile([P, P], F32, align_bytes=256)
         make_identity(nc, identity[:])
 
         norms = const.tile([P, P], F32)
@@ -114,7 +114,7 @@ def tile_candidateaware_clickednewsattention_pa_k_kernel(
                 nc.sync.dma_start(out=bias[:], in_=bq.partition_broadcast(P))
 
         def transpose(j):
-            x_sorted = work.tile([P, UNIT_GROUPS, 2, P], F32)
+            x_sorted = work.tile([P, UNIT_GROUPS, 2, P], F32, align_bytes=256)
             nc.vector.tensor_copy(
                 out=x_sorted[:],
                 in_=x_raw[j][:].bitcast(F32).rearrange("n (g p u) -> n g u p", g=UNIT_GROUPS, u=2),

@@ -66,7 +66,7 @@ def tile_candidateaware_clickednewsattention_pa_k_kernel(
         norms = const.tile([P, P], F32)
         nc.vector.memset(norms[:], 0.0)
         sum_squares = const.tile([P, USERS], F32)
-        bias = const.tile([P, FEATURES], BF16)
+        bias = const.tile([P, FEATURES], BF16, align_bytes=256)
         zeros = const.tile([P, FEATURES], BF16)
         nc.vector.memset(zeros[:], 0.0)
 
@@ -105,7 +105,7 @@ def tile_candidateaware_clickednewsattention_pa_k_kernel(
 
         def load(j):
             chunk, user = divmod(j, USERS)
-            raw = x_pool.tile([P, K_UNIT], BF16)
+            raw = x_pool.tile([P, K_UNIT], BF16, align_bytes=256)
             nc.sync.dma_start(out=raw[:], in_=cand_topics[user, :, chunk * K_UNIT : (chunk + 1) * K_UNIT])
             x_raw[j] = raw
             if user == USERS - 1:
@@ -157,10 +157,10 @@ def tile_candidateaware_clickednewsattention_pa_k_kernel(
                 )
 
         def finish(user):
-            q = results.tile([P, FEATURES], F32)
+            q = results.tile([P, FEATURES], F32, align_bytes=256)
             nc.vector.tensor_tensor(out=q[:], in0=q_sums[user][:], in1=bias[:], op=ALU.add)
             nc.sync.dma_start(out=out_0[user, :, :], in_=q[:])
-            squares = results.tile([P, FEATURES], F32)
+            squares = results.tile([P, FEATURES], F32, align_bytes=256)
             nc.scalar.activation(
                 out=squares[:], in_=q[:], func=ACT.Square, accum_out=sum_squares[:, user : user + 1]
             )

from contextlib import ExitStack

import concourse.mybir as mybir
from concourse.masks import make_identity

F32 = mybir.dt.float32
BF16 = mybir.dt.bfloat16
I32 = mybir.dt.int32
U32 = mybir.dt.uint32
U8 = mybir.dt.uint8
FP8X4 = mybir.dt.float8_e4m3fn_x4
FP4X4 = mybir.dt.float4_e2m1fn_x4
ACT = mybir.ActivationFunctionType
ALU = mybir.AluOpType
AXIS = mybir.AxisListType

P = 128
USERS = 4
K = 16384
FEATURES = 512
PACK = 4
K_GROUP = P * PACK
GROUPS = K // K_GROUP
SCALE_ROWS = K_GROUP // 32
QUADRANT = 32
QUADRANT_ROWS = SCALE_ROWS // (P // QUADRANT)

UNIT_GROUPS = 4
K_UNIT = UNIT_GROUPS * K_GROUP
CHUNKS = GROUPS // UNIT_GROUPS
UNITS = CHUNKS * USERS
BANK_GROUPS = 2
UNIT_BANKS = UNIT_GROUPS // BANK_GROUPS
RUN = 2
X_AHEAD = 14
WARM_FIRST = 6
WARM_BETWEEN = 2

FLOPS = 2 * USERS * P * K * FEATURES


def tile_candidateaware_clickednewsattention_pa_k_kernel(
    tc, cand_topics, Wq_words, Wq_scales, bq, out_0, out_1
):
    nc = tc.nc
    with ExitStack() as ctx:
        ctx.enter_context(tc.manual_schedule())
        const = ctx.enter_context(tc.tile_pool(name="const", bufs=1))
        weights = ctx.enter_context(tc.tile_pool(name="weights", bufs=1))
        x_pool = ctx.enter_context(tc.tile_pool(name="x", bufs=X_AHEAD + 1))
        work = ctx.enter_context(tc.tile_pool(name="work", bufs=2 * RUN))
        results = ctx.enter_context(tc.tile_pool(name="results", bufs=USERS))
        sums = ctx.enter_context(tc.psum_pool(name="sums", bufs=1))
        banks = ctx.enter_context(tc.psum_pool(name="banks", bufs=RUN * UNIT_BANKS))

        one = const.tile([P, 1], F32)
        nc.vector.memset(one[:], 1.0)
        table_warm = const.tile([P, 1], F32)
        nc.scalar.activation(out=table_warm[:], in_=one[:], func=ACT.Exp)
        half = const.tile([P, 1], F32)
        nc.vector.memset(half[:], 0.5)

        identity = const.tile([P, P], F32, align_bytes=256)
        make_identity(nc, identity[:])

        norms = const.tile([P, P], F32)
        nc.vector.memset(norms[:], 0.0)
        sum_squares = const.tile([P, USERS], F32)
        bias = const.tile([P, FEATURES], BF16, align_bytes=256)
        zeros = const.tile([P, FEATURES], BF16)
        nc.vector.memset(zeros[:], 0.0)

        q_sums = []
        for user in range(USERS):
            q_sum = sums.tile([P, FEATURES], F32, name="q_sum%d" % user)
            q_sums.append(q_sum)

        def keep_warm(count):
            for repeat in range(count):
                nc.tensor.matmul(out=q_sums[USERS - 1][:], lhsT=zeros[:, 0:P], rhs=zeros[:], start=True, stop=True)

        words_i32 = Wq_words.bitcast(I32)
        scales_i32 = Wq_scales.bitcast(I32)

        w_words = {}
        w_planes = {}
        x_raw = {}
        x_grouped = {}
        x_codes = {}
        x_planes = {}

        def load_weights(chunk):
            groups = slice(chunk * UNIT_GROUPS, (chunk + 1) * UNIT_GROUPS)
            words = weights.tile([P, UNIT_GROUPS, 2 * FEATURES], U8, name="w_words%d" % chunk, align_bytes=256)
            planes = weights.tile([P, UNIT_GROUPS, FEATURES], U8, name="w_planes%d" % chunk, align_bytes=256)
            nc.vector.memset(planes[:].bitcast(I32), 0)
            for r in range(QUADRANT_ROWS):
                nc.sync.dma_start(
                    out=planes[r:P:QUADRANT, :, :].bitcast(I32),
                    in_=scales_i32[groups, r:SCALE_ROWS:QUADRANT_ROWS, :].rearrange("g j n -> j g n"),
                )
            nc.sync.dma_start(out=words[:].bitcast(I32), in_=words_i32[groups, :, :].rearrange("g p b -> p g b"))
            w_words[chunk] = words
            w_planes[chunk] = planes

        def load(j):
            chunk, user = divmod(j, USERS)
            raw = x_pool.tile([P, K_UNIT], BF16, align_bytes=256)
            nc.sync.dma_start(out=raw[:], in_=cand_topics[user, :, chunk * K_UNIT : (chunk + 1) * K_UNIT])
            x_raw[j] = raw
            if user == USERS - 1:
                load_weights(chunk)
            if j == UNITS - 1:
                nc.sync.dma_start(out=bias[:], in_=bq.partition_broadcast(P))

        def transpose(j):
            x_sorted = work.tile([P, UNIT_GROUPS, 2, P], F32, align_bytes=256)
            nc.vector.tensor_copy(
                out=x_sorted[:],
                in_=x_raw[j][:].bitcast(F32).rearrange("n (g p u) -> n g u p", g=UNIT_GROUPS, u=2),
            )
            grouped = work.tile([P, UNIT_GROUPS * P * PACK], BF16, align_bytes=256)
            grouped_words = grouped[:].bitcast(F32).rearrange("p (g n u) -> p g n u", g=UNIT_GROUPS, u=2)
            for first_group in range(0, UNIT_GROUPS, BANK_GROUPS):
                bank = banks.tile([P, BANK_GROUPS, 2, P], F32, tag="bank")
                for g in range(BANK_GROUPS):
                    for u in range(2):
                        nc.tensor.transpose(
                            out=bank[:, g, u, :], in_=x_sorted[:, first_group + g, u, :], identity=identity[:]
                        )
                nc.scalar.copy(
                    out=grouped_words[:, first_group : first_group + BANK_GROUPS, :, :],
                    in_=bank[:].rearrange("p g u n -> p g n u"),
                )
            x_grouped[j] = grouped

        def quantise(j):
            codes = work.tile([P, UNIT_GROUPS * P], U32, align_bytes=256)
            planes = work.tile([P, UNIT_GROUPS * P], U8, align_bytes=256)
            nc.vector.quantize_mx(out=codes[:].bitcast(FP8X4), scales=planes[:], in_=x_grouped[j][:])
            x_codes[j] = codes
            x_planes[j] = planes

        def multiply(j):
            chunk, user = divmod(j, USERS)
            for g in range(UNIT_GROUPS):
                group = chunk * UNIT_GROUPS + g
                candidates = slice(g * P, (g + 1) * P)
                nc.tensor.matmul_mx(
                    out=q_sums[user][:],
                    lhsT=x_codes[j][:, candidates].bitcast(FP8X4),
                    lhsT_scale=x_planes[j][:, candidates],
                    rhs=w_words[chunk][:, g, :].bitcast(FP4X4),
                    rhs_scale=w_planes[chunk][:, g, :],
                    start=(group == 0),
                    stop=(group == GROUPS - 1),
                )

        def finish(user):
            q = results.tile([P, FEATURES], F32, align_bytes=256)
            nc.vector.tensor_tensor(out=q[:], in0=q_sums[user][:], in1=bias[:], op=ALU.add)
            nc.sync.dma_start(out=out_0[user, :, :], in_=q[:])
            squares = results.tile([P, FEATURES], F32, align_bytes=256)
            nc.scalar.activation(
                out=squares[:], in_=q[:], func=ACT.Square, accum_out=sum_squares[:, user : user + 1]
            )
            nc.gpsimd.tensor_tensor(
                out=norms[:, user : user + 1], in0=sum_squares[:, user : user + 1], in1=half[:], op=ALU.pow
            )

        def run_units(first):
            return [j for j in range(first, first + RUN) if 0 <= j < UNITS]

        for j in range(X_AHEAD):
            load(j)
        keep_warm(WARM_FIRST)
        for first in range(0, UNITS + 2 * RUN, RUN):
            for j in run_units(first):
                if j + X_AHEAD < UNITS:
                    load(j + X_AHEAD)
                transpose(j)
                if j < USERS:
                    keep_warm(WARM_BETWEEN)
            for j in run_units(first - RUN):
                quantise(j)
            for j in run_units(first - 2 * RUN):
                if j // USERS == CHUNKS - 1:
                    finish(j % USERS)
            for j in run_units(first - RUN):
                multiply(j)

        norms_bank = banks.tile([P, P], F32, tag="bank")
        nc.tensor.transpose(out=norms_bank[:], in_=norms[:], identity=identity[:])
        minus_top = const.tile([P, 1], F32)
        nc.vector.reduce_max(out=minus_top[:], in_=norms_bank[:], axis=AXIS.X, negate=True)
        powers = const.tile([P, P], F32)
        total = const.tile([P, 1], F32)
        nc.scalar.activation(
            out=powers[:], in_=norms_bank[:], func=ACT.Exp, bias=minus_top[:], scale=1.0, accum_out=total[:]
        )
        inverse = const.tile([P, 1], F32)
        nc.vector.reciprocal(out=inverse[:], in_=total[:])
        query_weights = const.tile([P, P], F32)
        nc.vector.tensor_scalar_mul(out=query_weights[:], in0=powers[:], scalar1=inverse[:])
        nc.sync.dma_start(out=out_1[:, :], in_=query_weights[0:USERS, :])
